import numpy as np
import ml_dtypes


def mxq(x, axis, fmt="e4m3"):
    dtype, down = {"e4m3": (ml_dtypes.float8_e4m3fn, 7), "e5m2": (ml_dtypes.float8_e5m2, 14)}[fmt]
    v = np.moveaxis(np.asarray(x, np.float32).astype(ml_dtypes.bfloat16).astype(np.float64), axis, -1)
    blocks = v.reshape(v.shape[:-1] + (-1, 32))
    amax = np.abs(blocks).max(-1, keepdims=True)
    byte = np.maximum(np.where(amax > 0, np.frexp(amax)[1] - 1 + 127, 0) - down, 1)
    scale = np.exp2(byte - 127.0)
    codes = (blocks / scale).astype(np.float32).astype(dtype).astype(np.float64)
    return np.moveaxis((codes * scale).reshape(v.shape), -1, axis)


WIDE = False


def mx_kscale(k):
    if not WIDE:
        return np.ones(k)
    levels = np.array([10, -10, 5, -5, 0])
    a = np.random.permutation(np.resize(levels, k // 512 * 4)).reshape(k // 512, 4)
    idx = np.arange(k)
    return np.exp2(a[idx // 512, idx % 128 // 32])


BF16 = ml_dtypes.bfloat16


def bf(x):
    return np.asarray(x, np.float32).astype(BF16)


def f64(x):
    return np.asarray(x).astype(np.float64)


B, S, D, O, BS = 4, 2048, 1024, 256, 256
MULT = D // BS


def fwht(x):
    n = x.shape[-1]
    steps = int(round(np.log2(n)))
    shape = x.shape
    x = x.reshape(-1, n)
    h = 1
    for _ in range(steps):
        x = x.reshape(-1, n // (2 * h), 2, h)
        a = x[:, :, 0, :]
        b = x[:, :, 1, :]
        x = np.stack([a + b, a - b], axis=2).reshape(-1, n)
        h *= 2
    return x.reshape(shape)


def pad_to_block_last(x, blocksize):
    size = x.shape[-1]
    target = ((size - 1) // blocksize + 1) * blocksize
    delta = target - size
    if delta == 0:
        return x
    pad = [(0, 0)] * (x.ndim - 1) + [(0, delta)]
    return np.pad(x, pad)


def block_factors():
    lv = np.unique(mx_kscale(D))
    lv = lv[np.argsort(-np.abs(np.log2(lv)), kind="stable")]
    return np.repeat(lv[np.arange(MULT) % len(lv)], BS)


def setup_inputs():
    s = block_factors()
    return {"input": bf(np.random.standard_normal((B, S, D)) * s),
            "weight": bf(np.random.standard_normal((O, D)) / np.sqrt(D) / s[None, :])}


def reference(input, weight):
    x = pad_to_block_last(f64(input), BS)
    lead = x.shape[:-1]
    d = x.shape[-1]
    mult = d // BS
    x = x.reshape(lead + (mult, BS))
    x = fwht(x) * (1.0 / np.sqrt(BS))
    x = x.reshape(lead + (d,))
    return mxq(x, 2, "e4m3") @ mxq(f64(weight), 1, "e4m3").T

@@ -1,0 +1,196 @@
+from contextlib import ExitStack
+
+import concourse.mybir as mybir
+from concourse.masks import make_identity
+
+F32 = mybir.dt.float32
+BF16 = mybir.dt.bfloat16
+U32 = mybir.dt.uint32
+U8 = mybir.dt.uint8
+FP8X4 = mybir.dt.float8_e4m3fn_x4
+ALU = mybir.AluOpType
+
+P = 128
+TOKENS = 8192
+D = 1024
+O = 256
+GROUP = 512
+TILES = GROUP // P
+N_GROUPS = TOKENS // GROUP
+COLS = TILES * D
+
+FLOPS = 2 * TOKENS * D * O + TOKENS * D * 8
+
+
+def minus(a, s):
+    both = a & s
+    return ((both >> 2) ^ (both >> 1) ^ both) & 1 == 1
+
+
+def tile_hadlinear_t_kernel(tc, x, weight, out):
+    nc = tc.nc
+    xv = x.flatten_outer_dims().rearrange("(G p j) f -> G p (j f)", p=P, j=TILES)
+    ov = out.flatten_outer_dims().rearrange("(G p j) o -> G p (j o)", p=P, j=TILES)
+
+    with ExitStack() as ctx:
+        const = ctx.enter_context(tc.tile_pool(name="const", bufs=1))
+        xpool = ctx.enter_context(tc.tile_pool(name="xpool", bufs=3))
+        stage = ctx.enter_context(tc.tile_pool(name="stage", bufs=1))
+        upool = ctx.enter_context(tc.tile_pool(name="upool", bufs=2))
+        work = ctx.enter_context(tc.tile_pool(name="work", bufs=2))
+        psum_y = ctx.enter_context(tc.psum_pool(name="psum_y", bufs=6))
+        psum_o = ctx.enter_context(tc.psum_pool(name="psum_o", bufs=2))
+
+        x_tiles = {}
+
+        def load_x(G):
+            x_sb = xpool.tile([P, COLS], BF16, name="x_sb")
+            nc.sync.dma_start(out=x_sb[:], in_=xv[G])
+            x_tiles[G] = x_sb
+
+        load_x(0)
+        w_sb = const.tile([P, 2 * D], BF16)
+        nc.scalar.dma_start(
+            out=w_sb[:].rearrange("p (a k) -> p a k", a=2),
+            in_=weight.rearrange("(a p) k -> p a k", p=P),
+        )
+        load_x(1)
+
+        ident = const.tile([P, P], F32)
+        make_identity(nc, ident[:])
+        ident_bf = const.tile([P, P], BF16)
+        make_identity(nc, ident_bf[:])
+
+        w_r = const.tile([P, 2 * D], BF16)
+        w_grp = const.tile([P, 2 * O * 4], BF16, align_bytes=64)
+        w_grp_v = w_grp[:].rearrange("p (g a o t) -> p g a o t", g=2, a=2, t=4)
+        for a in range(2):
+            nc.scalar.copy(
+                out=w_r[:, D * a : D * a + D].rearrange("p (c b l) -> p c b l", c=8, b=4),
+                in_=w_sb[:, D * a : D * a + D].rearrange("p (b c l) -> p c b l", c=8, b=4),
+            )
+            wt_ps = psum_o.tile([P, D], BF16, tag="o", name="wt_ps")
+            for c in range(8):
+                nc.tensor.transpose(
+                    wt_ps[:, P * c : P * c + P],
+                    w_r[:, D * a + P * c : D * a + P * c + P],
+                    ident_bf[:],
+                )
+            wt_v = wt_ps[:].rearrange("p (g t o) -> p g o t", g=2, t=4)
+            for g in range(2):
+                nc.scalar.copy(out=w_grp_v[:, g, a, :, :], in_=wt_v[:, g, :, :])
+        w_codes = const.tile([P, 2 * O], U32, align_bytes=64)
+        w_scales = const.tile([P, 2 * O], U8, align_bytes=64)
+        nc.vector.quantize_mx(out=w_codes[:].bitcast(FP8X4), scales=w_scales[:], in_=w_grp[:])
+
+        u_tiles = {}
+        grp_tiles = {}
+        code_tiles = {}
+        mid_tiles = {}
+
+        def pair_stage(dst, in0, in1):
+            halves = dst[:].rearrange("p (n b m) -> p n b m", b=2, m=16)
+            shape4 = "p (s q) m -> p s q m"
+            if len(in0.shape) == 4:
+                plus = halves[:, :, 0, :].rearrange(shape4, s=8)
+                less = halves[:, :, 1, :].rearrange(shape4, s=8)
+            else:
+                plus = halves[:, :, 0, :]
+                less = halves[:, :, 1, :]
+            nc.vector.tensor_tensor(out=plus, in0=in0, in1=in1, op=ALU.add)
+            nc.vector.tensor_tensor(out=less, in0=in0, in1=in1, op=ALU.subtract)
+
+        def first_stage(G):
+            xin = x_tiles[G][:].rearrange("p (q s m two) -> p s q m two", q=16, s=8, two=2)
+            buf_a = stage.tile([P, COLS], F32, name="buf_a")
+            pair_stage(buf_a, xin[:, :, :, :, 0], xin[:, :, :, :, 1])
+            mid_tiles[G] = buf_a
+
+        def other_stages(G):
+            src = mid_tiles[G]
+            for st in range(4):
+                if st == 3:
+                    dst = upool.tile([P, COLS], F32, name="u_pos")
+                elif st % 2 == 0:
+                    dst = stage.tile([P, COLS], F32, name="buf_b")
+                else:
+                    dst = stage.tile([P, COLS], F32, name="buf_a")
+                pairs = src[:].rearrange("p (n m two) -> p n m two", m=16, two=2)
+                pair_stage(dst, pairs[:, :, :, 0], pairs[:, :, :, 1])
+                src = dst
+            u_neg = upool.tile([P, COLS - GROUP], F32, name="u_neg")
+            for piece in range(7):
+                nc.scalar.mul(
+                    out=u_neg[:, GROUP * piece : GROUP * piece + GROUP],
+                    in_=src[:, GROUP * (piece + 1) : GROUP * (piece + 2)],
+                    mul=-1.0,
+                )
+            u_tiles[G] = (src, u_neg)
+
+        def adding_transposes(G):
+            u_pos, u_neg = u_tiles[G]
+            grp = work.tile([P, COLS], BF16, name="grp", align_bytes=64)
+            grp_v = grp[:].rearrange("p (j g m t) -> p j g m t", j=TILES, g=2, t=4)
+            for j in range(TILES):
+                for g in range(2):
+                    y_ps = psum_y.tile([P, 512], F32, tag="y", name="y_ps")
+                    for t in range(4):
+                        for s in range(8):
+                            if minus(4 * g + t, s):
+                                part = u_neg[:, GROUP * (s - 1) + P * j : GROUP * (s - 1) + P * j + P]
+                            else:
+                                part = u_pos[:, GROUP * s + P * j : GROUP * s + P * j + P]
+                            nc.tensor.matmul(
+                                out=y_ps[:, P * t : P * t + P],
+                                lhsT=part,
+                                rhs=ident[:],
+                                is_transpose=True,
+                                start=(s == 0),
+                                stop=(s == 7),
+                            )
+                    nc.scalar.mul(
+                        out=grp_v[:, j, g, :, :],
+                        in_=y_ps[:].rearrange("p (t m) -> p m t", t=4),
+                        mul=0.0625,
+                    )
+            grp_tiles[G] = grp
+
+        def quantise(G):
+            codes = work.tile([P, COLS // 4], U32, name="codes", align_bytes=64)
+            scales = work.tile([P, COLS // 4], U8, name="scales", align_bytes=64)
+            nc.vector.quantize_mx(
+                out=codes[:].bitcast(FP8X4), scales=scales[:], in_=grp_tiles[G][:]
+            )
+            code_tiles[G] = (codes, scales)
+
+        def linear(G):
+            codes, scales = code_tiles[G]
+            res = work.tile([P, TILES * O], F32, name="res")
+            for c in range(2):
+                o_ps = psum_o.tile([P, 512], F32, tag="o", name="o_ps")
+                for jj in range(2):
+                    for g in range(2):
+                        col = 256 * (2 * c + jj) + P * g
+                        nc.tensor.matmul_mx(
+                            out=o_ps[:, O * jj : O * jj + O],
+                            lhsT=codes[:, col : col + P].bitcast(FP8X4),
+                            lhsT_scale=scales[:, col : col + P],
+                            rhs=w_codes[:, O * g : O * g + O].bitcast(FP8X4),
+                            rhs_scale=w_scales[:, O * g : O * g + O],
+                            start=(g == 0),
+                            stop=(g == 1),
+                        )
+                nc.scalar.copy(out=res[:, 512 * c : 512 * c + 512], in_=o_ps[:])
+            nc.sync.dma_start(out=ov[G], in_=res[:])
+
+        for G in range(N_GROUPS + 2):
+            if G + 2 < N_GROUPS:
+                load_x(G + 2)
+            if G < N_GROUPS:
+                first_stage(G)
+            if G >= 2:
+                quantise(G - 2)
+                linear(G - 2)
+            if G < N_GROUPS:
+                other_stages(G)
+                adding_transposes(G)

@@ -21,6 +21,8 @@ COLS = TILES * D
 
 FLOPS = 2 * TOKENS * D * O + TOKENS * D * 8
 
+EXTRA = [0, 0, 1, 0, 0, 0, 1, 0, 0, 0, 1, 0, 0, 1, 0, 2]
+
 
 def minus(a, s):
     both = a & s
@@ -108,45 +110,58 @@ def tile_hadlinear_t_kernel(tc, x, weight, out):
 
         def other_stages(G):
             src = mid_tiles[G]
-            for st in range(4):
-                if st == 3:
+            extra = EXTRA[G]
+            for st in range(4 + extra):
+                if st == 3 + extra:
                     dst = upool.tile([P, COLS], F32, name="u_pos")
                 elif st % 2 == 0:
                     dst = stage.tile([P, COLS], F32, name="buf_b")
                 else:
                     dst = stage.tile([P, COLS], F32, name="buf_a")
-                pairs = src[:].rearrange("p (n m two) -> p n m two", m=16, two=2)
-                pair_stage(dst, pairs[:, :, :, 0], pairs[:, :, :, 1])
+                if st < 4:
+                    pairs = src[:].rearrange("p (n m two) -> p n m two", m=16, two=2)
+                    pair_stage(dst, pairs[:, :, :, 0], pairs[:, :, :, 1])
+                else:
+                    run = GROUP << (st - 4)
+                    sv = src[:].rearrange("p (h two c) -> p h two c", two=2, c=run)
+                    dv = dst[:].rearrange("p (h two c) -> p h two c", two=2, c=run)
+                    nc.vector.tensor_tensor(
+                        out=dv[:, :, 0, :], in0=sv[:, :, 0, :], in1=sv[:, :, 1, :], op=ALU.add
+                    )
+                    nc.vector.tensor_tensor(
+                        out=dv[:, :, 1, :], in0=sv[:, :, 0, :], in1=sv[:, :, 1, :], op=ALU.subtract
+                    )
                 src = dst
-            u_neg = upool.tile([P, COLS - GROUP], F32, name="u_neg")
-            for piece in range(7):
+            u_neg = upool.tile([P, COLS], F32, name="u_neg")
+            for s8 in range(1 << extra, 8):
                 nc.scalar.mul(
-                    out=u_neg[:, GROUP * piece : GROUP * piece + GROUP],
-                    in_=src[:, GROUP * (piece + 1) : GROUP * (piece + 2)],
+                    out=u_neg[:, GROUP * s8 : GROUP * s8 + GROUP],
+                    in_=src[:, GROUP * s8 : GROUP * s8 + GROUP],
                     mul=-1.0,
                 )
             u_tiles[G] = (src, u_neg)
 
         def adding_transposes(G):
             u_pos, u_neg = u_tiles[G]
+            extra = EXTRA[G]
+            terms = 8 >> extra
             grp = work.tile([P, COLS], BF16, name="grp", align_bytes=64)
             grp_v = grp[:].rearrange("p (j g m t) -> p j g m t", j=TILES, g=2, t=4)
             for j in range(TILES):
                 for g in range(2):
                     y_ps = psum_y.tile([P, 512], F32, tag="y", name="y_ps")
                     for t in range(4):
-                        for s in range(8):
-                            if minus(4 * g + t, s):
-                                part = u_neg[:, GROUP * (s - 1) + P * j : GROUP * (s - 1) + P * j + P]
-                            else:
-                                part = u_pos[:, GROUP * s + P * j : GROUP * s + P * j + P]
+                        a8 = 4 * g + t
+                        for sg in range(terms):
+                            s8 = (sg << extra) | (a8 & ((1 << extra) - 1))
+                            part = u_neg if minus(a8 >> extra, sg) else u_pos
                             nc.tensor.matmul(
                                 out=y_ps[:, P * t : P * t + P],
-                                lhsT=part,
+                                lhsT=part[:, GROUP * s8 + P * j : GROUP * s8 + P * j + P],
                                 rhs=ident[:],
                                 is_transpose=True,
-                                start=(s == 0),
-                                stop=(s == 7),
+                                start=(sg == 0),
+                                stop=(sg == terms - 1),
                             )
                     nc.scalar.mul(
                         out=grp_v[:, j, g, :, :],

@@ -21,7 +21,8 @@ COLS = TILES * D
 
 FLOPS = 2 * TOKENS * D * O + TOKENS * D * 8
 
-EXTRA = [0, 0, 1, 0, 0, 0, 1, 0, 0, 0, 1, 0, 0, 1, 0, 2]
+N_MATMUL = 3
+EXTRA = [0, 0, 0, 0, 0, 0, 1, 0, 0, 0, 0, 0, 2]
 
 
 def minus(a, s):
@@ -36,20 +37,23 @@ def tile_hadlinear_t_kernel(tc, x, weight, out):
 
     with ExitStack() as ctx:
         const = ctx.enter_context(tc.tile_pool(name="const", bufs=1))
-        xpool = ctx.enter_context(tc.tile_pool(name="xpool", bufs=3))
+        xpool = ctx.enter_context(tc.tile_pool(name="xpool", bufs=4))
         stage = ctx.enter_context(tc.tile_pool(name="stage", bufs=1))
-        upool = ctx.enter_context(tc.tile_pool(name="upool", bufs=2))
+        upool = ctx.enter_context(tc.tile_pool(name="upool", bufs=3))
+        gpool = ctx.enter_context(tc.tile_pool(name="gpool", bufs=3))
         work = ctx.enter_context(tc.tile_pool(name="work", bufs=2))
         psum_y = ctx.enter_context(tc.psum_pool(name="psum_y", bufs=6))
         psum_o = ctx.enter_context(tc.psum_pool(name="psum_o", bufs=2))
+        ctx.enter_context(tc.manual_schedule())
 
         x_tiles = {}
 
-        def load_x(G):
+        def load_x(slot):
             x_sb = xpool.tile([P, COLS], BF16, name="x_sb")
-            nc.sync.dma_start(out=x_sb[:], in_=xv[G])
-            x_tiles[G] = x_sb
+            nc.sync.dma_start(out=x_sb[:], in_=xv[slot])
+            x_tiles[slot] = x_sb
 
+        load_x(N_MATMUL)
         load_x(0)
         w_sb = const.tile([P, 2 * D], BF16)
         nc.scalar.dma_start(
@@ -57,11 +61,186 @@ def tile_hadlinear_t_kernel(tc, x, weight, out):
             in_=weight.rearrange("(a p) k -> p a k", p=P),
         )
         load_x(1)
+        load_x(2)
 
         ident = const.tile([P, P], F32)
         make_identity(nc, ident[:])
         ident_bf = const.tile([P, P], BF16)
         make_identity(nc, ident_bf[:])
+
+        h_src = ident
+        for st in range(7):
+            h_dst = const.tile([P, P], F32, name="h_%d" % (st % 2))
+            hp = h_src[:].rearrange("p (m two) -> p m two", two=2)
+            nc.vector.tensor_tensor(out=h_dst[:, 0:64], in0=hp[:, :, 0], in1=hp[:, :, 1], op=ALU.add)
+            nc.vector.tensor_tensor(
+                out=h_dst[:, 64:128], in0=hp[:, :, 0], in1=hp[:, :, 1], op=ALU.subtract
+            )
+            h_src = h_dst
+        h128 = const.tile([P, P], BF16)
+        nc.vector.tensor_copy(out=h128[:], in_=h_src[:])
+
+        u_tiles = {}
+        grp_tiles = {}
+        code_tiles = {}
+        mid_tiles = {}
+
+        def pair_stage(dst, in0, in1):
+            halves = dst[:].rearrange("p (n b m) -> p n b m", b=2, m=16)
+            shape4 = "p (s q) m -> p s q m"
+            if len(in0.shape) == 4:
+                plus = halves[:, :, 0, :].rearrange(shape4, s=8)
+                less = halves[:, :, 1, :].rearrange(shape4, s=8)
+            else:
+                plus = halves[:, :, 0, :]
+                less = halves[:, :, 1, :]
+            nc.vector.tensor_tensor(out=plus, in0=in0, in1=in1, op=ALU.add)
+            nc.vector.tensor_tensor(out=less, in0=in0, in1=in1, op=ALU.subtract)
+
+        def vector_stages(slot, first, last):
+            extra = EXTRA[slot - N_MATMUL]
+            for st in range(first, last):
+                if st == 4 + extra:
+                    dst = upool.tile([P, COLS], F32, name="u_pos")
+                elif st % 2 == 0:
+                    dst = stage.tile([P, COLS], F32, name="buf_a")
+                else:
+                    dst = stage.tile([P, COLS], F32, name="buf_b")
+                if st == 0:
+                    xin = x_tiles[slot][:].rearrange(
+                        "p (q s m two) -> p s q m two", q=16, s=8, two=2
+                    )
+                    pair_stage(dst, xin[:, :, :, :, 0], xin[:, :, :, :, 1])
+                elif st < 5:
+                    pairs = mid_tiles[slot][:].rearrange("p (n m two) -> p n m two", m=16, two=2)
+                    pair_stage(dst, pairs[:, :, :, 0], pairs[:, :, :, 1])
+                else:
+                    run = GROUP << (st - 5)
+                    sv = mid_tiles[slot][:].rearrange("p (h two c) -> p h two c", two=2, c=run)
+                    dv = dst[:].rearrange("p (h two c) -> p h two c", two=2, c=run)
+                    nc.vector.tensor_tensor(
+                        out=dv[:, :, 0, :], in0=sv[:, :, 0, :], in1=sv[:, :, 1, :], op=ALU.add
+                    )
+                    nc.vector.tensor_tensor(
+                        out=dv[:, :, 1, :], in0=sv[:, :, 0, :], in1=sv[:, :, 1, :], op=ALU.subtract
+                    )
+                mid_tiles[slot] = dst
+
+        def negate(slot):
+            extra = EXTRA[slot - N_MATMUL]
+            u_pos = mid_tiles[slot]
+            u_neg = upool.tile([P, COLS], F32, name="u_neg")
+            for s8 in range(1 << extra, 8):
+                nc.scalar.mul(
+                    out=u_neg[:, GROUP * s8 : GROUP * s8 + GROUP],
+                    in_=u_pos[:, GROUP * s8 : GROUP * s8 + GROUP],
+                    mul=-1.0,
+                )
+            u_tiles[slot] = (u_pos, u_neg, extra)
+
+        def matmul_road(slot):
+            x_sb = x_tiles[slot]
+            u_pos = upool.tile([P, COLS], F32, name="u_pos")
+            u_neg = upool.tile([P, COLS], F32, name="u_neg")
+            up_v = u_pos[:].rearrange("p (s j c) -> p s j c", s=8, j=TILES)
+            un_v = u_neg[:].rearrange("p (s j c) -> p s j c", s=8, j=TILES)
+            xt_tiles = {}
+
+            def transposes(j):
+                xt_ps = psum_y.tile([P, D], BF16, tag="y", name="xt_ps")
+                for c in range(8):
+                    nc.tensor.transpose(
+                        xt_ps[:, P * c : P * c + P],
+                        x_sb[:, D * j + P * c : D * j + P * c + P],
+                        ident_bf[:],
+                    )
+                xT_new = work.tile([P, D], BF16, name="xT")
+                nc.scalar.copy(out=xT_new[:], in_=xt_ps[:])
+                xt_tiles[j] = xT_new
+
+            transposes(0)
+            for j in range(TILES):
+                if j + 1 < TILES:
+                    transposes(j + 1)
+                xT = xt_tiles[j]
+                for top in range(2):
+                    z_ps = psum_y.tile([P, 512], F32, tag="y", name="z_ps")
+                    z_v = z_ps[:].rearrange("p (c b l) -> p c b l", c=4, b=4)
+                    for b in range(4):
+                        nc.tensor.matmul(
+                            out=z_v[:, :, b, :],
+                            lhsT=xT[:, P * (2 * b + top) : P * (2 * b + top) + P],
+                            rhs=h128[:],
+                            start=True,
+                            stop=True,
+                        )
+                    z_c = z_ps[:].rearrange("p (c r) -> p c r", c=4)
+                    nc.scalar.copy(out=up_v[:, 4 * top : 4 * top + 4, j, :], in_=z_c)
+                    if top == 1:
+                        nc.scalar.mul(out=un_v[:, 4:8, j, :], in_=z_c, mul=-1.0)
+            u_tiles[slot] = (u_pos, u_neg, 2)
+
+        def adding_transposes(slot, follower):
+            u_pos, u_neg, extra = u_tiles[slot]
+            terms = 8 >> extra
+            grp = gpool.tile([P, COLS], BF16, name="grp", align_bytes=64)
+            grp_v = grp[:].rearrange("p (j g m t) -> p j g m t", j=TILES, g=2, t=4)
+            for j in range(TILES):
+                banks = [psum_y.tile([P, 512], F32, tag="y", name="y_ps%d" % g) for g in range(2)]
+                for t in range(4):
+                    for sg in range(terms):
+                        for g in range(2):
+                            a8 = 4 * g + t
+                            s8 = (sg << extra) | (a8 & ((1 << extra) - 1))
+                            part = u_neg if minus(a8 >> extra, sg) else u_pos
+                            nc.tensor.matmul(
+                                out=banks[g][:, P * t : P * t + P],
+                                lhsT=part[:, GROUP * s8 + P * j : GROUP * s8 + P * j + P],
+                                rhs=ident[:],
+                                is_transpose=True,
+                                start=(sg == 0),
+                                stop=(sg == terms - 1),
+                            )
+                for g in range(2):
+                    nc.scalar.mul(
+                        out=grp_v[:, j, g, :, :],
+                        in_=banks[g][:].rearrange("p (t m) -> p m t", t=4),
+                        mul=0.0625,
+                    )
+                if j == 1 and follower is not None:
+                    negate(follower)
+            grp_tiles[slot] = grp
+
+        def quantise(slot):
+            codes = work.tile([P, COLS // 4], U32, name="codes", align_bytes=64)
+            scales = work.tile([P, COLS // 4], U8, name="scales", align_bytes=64)
+            nc.vector.quantize_mx(
+                out=codes[:].bitcast(FP8X4), scales=scales[:], in_=grp_tiles[slot][:]
+            )
+            code_tiles[slot] = (codes, scales)
+
+        def linear(slot):
+            codes, scales = code_tiles[slot]
+            res = work.tile([P, TILES * O], F32, name="res")
+            for c in range(2):
+                o_ps = psum_o.tile([P, 512], F32, tag="o", name="o_ps")
+                for jj in range(2):
+                    for g in range(2):
+                        col = 256 * (2 * c + jj) + P * g
+                        nc.tensor.matmul_mx(
+                            out=o_ps[:, O * jj : O * jj + O],
+                            lhsT=codes[:, col : col + P].bitcast(FP8X4),
+                            lhsT_scale=scales[:, col : col + P],
+                            rhs=w_codes[:, O * g : O * g + O].bitcast(FP8X4),
+                            rhs_scale=w_scales[:, O * g : O * g + O],
+                            start=(g == 0),
+                            stop=(g == 1),
+                        )
+                nc.scalar.copy(out=res[:, 512 * c : 512 * c + 512], in_=o_ps[:])
+            nc.sync.dma_start(out=ov[slot], in_=res[:])
+
+        first = N_MATMUL
+        vector_stages(first, 0, 4)
 
         w_r = const.tile([P, 2 * D], BF16)
         w_grp = const.tile([P, 2 * O * 4], BF16, align_bytes=64)
@@ -83,129 +262,32 @@ def tile_hadlinear_t_kernel(tc, x, weight, out):
                 nc.scalar.copy(out=w_grp_v[:, g, a, :, :], in_=wt_v[:, g, :, :])
         w_codes = const.tile([P, 2 * O], U32, align_bytes=64)
         w_scales = const.tile([P, 2 * O], U8, align_bytes=64)
+
+        for slot in range(N_MATMUL):
+            matmul_road(slot)
+            adding_transposes(slot, None)
+        load_x(first + 1)
+        vector_stages(first, 4, 5 + EXTRA[0])
         nc.vector.quantize_mx(out=w_codes[:].bitcast(FP8X4), scales=w_scales[:], in_=w_grp[:])
+        negate(first)
 
-        u_tiles = {}
-        grp_tiles = {}
-        code_tiles = {}
-        mid_tiles = {}
-
-        def pair_stage(dst, in0, in1):
-            halves = dst[:].rearrange("p (n b m) -> p n b m", b=2, m=16)
-            shape4 = "p (s q) m -> p s q m"
-            if len(in0.shape) == 4:
-                plus = halves[:, :, 0, :].rearrange(shape4, s=8)
-                less = halves[:, :, 1, :].rearrange(shape4, s=8)
+        for k in range(N_GROUPS - 1):
+            slot = first + k
+            nxt = slot + 1
+            if nxt + 1 < N_GROUPS:
+                load_x(nxt + 1)
+            if nxt < N_GROUPS:
+                vector_stages(nxt, 0, 1)
+            if k == 0:
+                ready = [0]
+            elif k == 1:
+                ready = [1, 2]
             else:
-                plus = halves[:, :, 0, :]
-                less = halves[:, :, 1, :]
-            nc.vector.tensor_tensor(out=plus, in0=in0, in1=in1, op=ALU.add)
-            nc.vector.tensor_tensor(out=less, in0=in0, in1=in1, op=ALU.subtract)
-
-        def first_stage(G):
-            xin = x_tiles[G][:].rearrange("p (q s m two) -> p s q m two", q=16, s=8, two=2)
-            buf_a = stage.tile([P, COLS], F32, name="buf_a")
-            pair_stage(buf_a, xin[:, :, :, :, 0], xin[:, :, :, :, 1])
-            mid_tiles[G] = buf_a
-
-        def other_stages(G):
-            src = mid_tiles[G]
-            extra = EXTRA[G]
-            for st in range(4 + extra):
-                if st == 3 + extra:
-                    dst = upool.tile([P, COLS], F32, name="u_pos")
-                elif st % 2 == 0:
-                    dst = stage.tile([P, COLS], F32, name="buf_b")
-                else:
-                    dst = stage.tile([P, COLS], F32, name="buf_a")
-                if st < 4:
-                    pairs = src[:].rearrange("p (n m two) -> p n m two", m=16, two=2)
-                    pair_stage(dst, pairs[:, :, :, 0], pairs[:, :, :, 1])
-                else:
-                    run = GROUP << (st - 4)
-                    sv = src[:].rearrange("p (h two c) -> p h two c", two=2, c=run)
-                    dv = dst[:].rearrange("p (h two c) -> p h two c", two=2, c=run)
-                    nc.vector.tensor_tensor(
-                        out=dv[:, :, 0, :], in0=sv[:, :, 0, :], in1=sv[:, :, 1, :], op=ALU.add
-                    )
-                    nc.vector.tensor_tensor(
-                        out=dv[:, :, 1, :], in0=sv[:, :, 0, :], in1=sv[:, :, 1, :], op=ALU.subtract
-                    )
-                src = dst
-            u_neg = upool.tile([P, COLS], F32, name="u_neg")
-            for s8 in range(1 << extra, 8):
-                nc.scalar.mul(
-                    out=u_neg[:, GROUP * s8 : GROUP * s8 + GROUP],
-                    in_=src[:, GROUP * s8 : GROUP * s8 + GROUP],
-                    mul=-1.0,
-                )
-            u_tiles[G] = (src, u_neg)
-
-        def adding_transposes(G):
-            u_pos, u_neg = u_tiles[G]
-            extra = EXTRA[G]
-            terms = 8 >> extra
-            grp = work.tile([P, COLS], BF16, name="grp", align_bytes=64)
-            grp_v = grp[:].rearrange("p (j g m t) -> p j g m t", j=TILES, g=2, t=4)
-            for j in range(TILES):
-                for g in range(2):
-                    y_ps = psum_y.tile([P, 512], F32, tag="y", name="y_ps")
-                    for t in range(4):
-                        a8 = 4 * g + t
-                        for sg in range(terms):
-                            s8 = (sg << extra) | (a8 & ((1 << extra) - 1))
-                            part = u_neg if minus(a8 >> extra, sg) else u_pos
-                            nc.tensor.matmul(
-                                out=y_ps[:, P * t : P * t + P],
-                                lhsT=part[:, GROUP * s8 + P * j : GROUP * s8 + P * j + P],
-                                rhs=ident[:],
-                                is_transpose=True,
-                                start=(sg == 0),
-                                stop=(sg == terms - 1),
-                            )
-                    nc.scalar.mul(
-                        out=grp_v[:, j, g, :, :],
-                        in_=y_ps[:].rearrange("p (t m) -> p m t", t=4),
-                        mul=0.0625,
-                    )
-            grp_tiles[G] = grp
-
-        def quantise(G):
-            codes = work.tile([P, COLS // 4], U32, name="codes", align_bytes=64)
-            scales = work.tile([P, COLS // 4], U8, name="scales", align_bytes=64)
-            nc.vector.quantize_mx(
-                out=codes[:].bitcast(FP8X4), scales=scales[:], in_=grp_tiles[G][:]
-            )
-            code_tiles[G] = (codes, scales)
-
-        def linear(G):
-            codes, scales = code_tiles[G]
-            res = work.tile([P, TILES * O], F32, name="res")
-            for c in range(2):
-                o_ps = psum_o.tile([P, 512], F32, tag="o", name="o_ps")
-                for jj in range(2):
-                    for g in range(2):
-                        col = 256 * (2 * c + jj) + P * g
-                        nc.tensor.matmul_mx(
-                            out=o_ps[:, O * jj : O * jj + O],
-                            lhsT=codes[:, col : col + P].bitcast(FP8X4),
-                            lhsT_scale=scales[:, col : col + P],
-                            rhs=w_codes[:, O * g : O * g + O].bitcast(FP8X4),
-                            rhs_scale=w_scales[:, O * g : O * g + O],
-                            start=(g == 0),
-                            stop=(g == 1),
-                        )
-                nc.scalar.copy(out=res[:, 512 * c : 512 * c + 512], in_=o_ps[:])
-            nc.sync.dma_start(out=ov[G], in_=res[:])
-
-        for G in range(N_GROUPS + 2):
-            if G + 2 < N_GROUPS:
-                load_x(G + 2)
-            if G < N_GROUPS:
-                first_stage(G)
-            if G >= 2:
-                quantise(G - 2)
-                linear(G - 2)
-            if G < N_GROUPS:
-                other_stages(G)
-                adding_transposes(G)
+                ready = [k + 1]
+            for done in ready:
+                quantise(done)
+                linear(done)
+            if nxt < N_GROUPS:
+                vector_stages(nxt, 1, 5 + EXTRA[nxt - N_MATMUL])
+            if slot < N_GROUPS:
+                adding_transposes(slot, nxt if nxt < N_GROUPS else None)

@@ -21,8 +21,14 @@ COLS = TILES * D
 
 FLOPS = 2 * TOKENS * D * O + TOKENS * D * 8
 
-N_MATMUL = 3
-EXTRA = [0, 0, 0, 0, 0, 0, 1, 0, 0, 0, 0, 0, 2]
+MATMUL_SLOTS = [(0, 0, 4, None), (1, 0, 4, None), (2, 0, 4, None)]
+ADD_SLOTS = [(G, 0, 4, 0) for G in range(3, 15)] + [
+    (15, 0, 1, 0),
+    (15, 1, 1, 0),
+    (15, 2, 1, 1),
+    (15, 3, 1, 2),
+]
+SLOTS = MATMUL_SLOTS + ADD_SLOTS
 
 
 def minus(a, s):
@@ -34,6 +40,8 @@ def tile_hadlinear_t_kernel(tc, x, weight, out):
     nc = tc.nc
     xv = x.flatten_outer_dims().rearrange("(G p j) f -> G p (j f)", p=P, j=TILES)
     ov = out.flatten_outer_dims().rearrange("(G p j) o -> G p (j o)", p=P, j=TILES)
+    n_mm = len(MATMUL_SLOTS)
+    n_slots = len(SLOTS)
 
     with ExitStack() as ctx:
         const = ctx.enter_context(tc.tile_pool(name="const", bufs=1))
@@ -47,13 +55,20 @@ def tile_hadlinear_t_kernel(tc, x, weight, out):
         ctx.enter_context(tc.manual_schedule())
 
         x_tiles = {}
+        mid_tiles = {}
+        u_tiles = {}
+        grp_tiles = {}
+        code_tiles = {}
 
-        def load_x(slot):
+        def load_x(i):
+            if i >= n_slots:
+                return
+            G, j0, n, extra = SLOTS[i]
             x_sb = xpool.tile([P, COLS], BF16, name="x_sb")
-            nc.sync.dma_start(out=x_sb[:], in_=xv[slot])
-            x_tiles[slot] = x_sb
+            nc.sync.dma_start(out=x_sb[:, : n * D], in_=xv[G][:, j0 * D : (j0 + n) * D])
+            x_tiles[i] = x_sb
 
-        load_x(N_MATMUL)
+        load_x(n_mm)
         load_x(0)
         w_sb = const.tile([P, 2 * D], BF16)
         nc.scalar.dma_start(
@@ -80,66 +95,60 @@ def tile_hadlinear_t_kernel(tc, x, weight, out):
         h128 = const.tile([P, P], BF16)
         nc.vector.tensor_copy(out=h128[:], in_=h_src[:])
 
-        u_tiles = {}
-        grp_tiles = {}
-        code_tiles = {}
-        mid_tiles = {}
-
-        def pair_stage(dst, in0, in1):
-            halves = dst[:].rearrange("p (n b m) -> p n b m", b=2, m=16)
-            shape4 = "p (s q) m -> p s q m"
-            if len(in0.shape) == 4:
-                plus = halves[:, :, 0, :].rearrange(shape4, s=8)
-                less = halves[:, :, 1, :].rearrange(shape4, s=8)
-            else:
-                plus = halves[:, :, 0, :]
-                less = halves[:, :, 1, :]
+        def add_and_subtract(plus, less, in0, in1):
             nc.vector.tensor_tensor(out=plus, in0=in0, in1=in1, op=ALU.add)
             nc.vector.tensor_tensor(out=less, in0=in0, in1=in1, op=ALU.subtract)
 
-        def vector_stages(slot, first, last):
-            extra = EXTRA[slot - N_MATMUL]
-            for st in range(first, last):
+        def vector_stages(i, first, last):
+            if i >= n_slots:
+                return
+            G, j0, n, extra = SLOTS[i]
+            cols = n * D
+            for st in range(first, min(last, 5 + extra)):
                 if st == 4 + extra:
                     dst = upool.tile([P, COLS], F32, name="u_pos")
                 elif st % 2 == 0:
                     dst = stage.tile([P, COLS], F32, name="buf_a")
                 else:
                     dst = stage.tile([P, COLS], F32, name="buf_b")
-                if st == 0:
-                    xin = x_tiles[slot][:].rearrange(
-                        "p (q s m two) -> p s q m two", q=16, s=8, two=2
-                    )
-                    pair_stage(dst, xin[:, :, :, :, 0], xin[:, :, :, :, 1])
-                elif st < 5:
-                    pairs = mid_tiles[slot][:].rearrange("p (n m two) -> p n m two", m=16, two=2)
-                    pair_stage(dst, pairs[:, :, :, 0], pairs[:, :, :, 1])
+                if st < 5:
+                    halves = dst[:, :cols].rearrange("p (r b m) -> p r b m", b=2, m=16)
+                    if st == 0:
+                        pairs = x_tiles[i][:, :cols].rearrange(
+                            "p (q s m two) -> p s q m two", s=8, m=16, two=2
+                        )
+                        add_and_subtract(
+                            halves[:, :, 0, :].rearrange("p (s q) m -> p s q m", s=8),
+                            halves[:, :, 1, :].rearrange("p (s q) m -> p s q m", s=8),
+                            pairs[:, :, :, :, 0],
+                            pairs[:, :, :, :, 1],
+                        )
+                    else:
+                        pairs = mid_tiles[i][:, :cols].rearrange(
+                            "p (r m two) -> p r m two", m=16, two=2
+                        )
+                        add_and_subtract(
+                            halves[:, :, 0, :], halves[:, :, 1, :], pairs[:, :, :, 0], pairs[:, :, :, 1]
+                        )
                 else:
-                    run = GROUP << (st - 5)
-                    sv = mid_tiles[slot][:].rearrange("p (h two c) -> p h two c", two=2, c=run)
-                    dv = dst[:].rearrange("p (h two c) -> p h two c", two=2, c=run)
-                    nc.vector.tensor_tensor(
-                        out=dv[:, :, 0, :], in0=sv[:, :, 0, :], in1=sv[:, :, 1, :], op=ALU.add
-                    )
-                    nc.vector.tensor_tensor(
-                        out=dv[:, :, 1, :], in0=sv[:, :, 0, :], in1=sv[:, :, 1, :], op=ALU.subtract
-                    )
-                mid_tiles[slot] = dst
+                    run = (n * P) << (st - 5)
+                    sv = mid_tiles[i][:, :cols].rearrange("p (h two c) -> p h two c", two=2, c=run)
+                    dv = dst[:, :cols].rearrange("p (h two c) -> p h two c", two=2, c=run)
+                    add_and_subtract(dv[:, :, 0, :], dv[:, :, 1, :], sv[:, :, 0, :], sv[:, :, 1, :])
+                mid_tiles[i] = dst
 
-        def negate(slot):
-            extra = EXTRA[slot - N_MATMUL]
-            u_pos = mid_tiles[slot]
+        def negate(i):
+            G, j0, n, extra = SLOTS[i]
+            width = n * P
+            u_pos = mid_tiles[i]
             u_neg = upool.tile([P, COLS], F32, name="u_neg")
-            for s8 in range(1 << extra, 8):
-                nc.scalar.mul(
-                    out=u_neg[:, GROUP * s8 : GROUP * s8 + GROUP],
-                    in_=u_pos[:, GROUP * s8 : GROUP * s8 + GROUP],
-                    mul=-1.0,
-                )
-            u_tiles[slot] = (u_pos, u_neg, extra)
+            for lo in range(width << extra, 8 * width, 512):
+                hi = min(lo + 512, 8 * width)
+                nc.scalar.mul(out=u_neg[:, lo:hi], in_=u_pos[:, lo:hi], mul=-1.0)
+            u_tiles[i] = (u_pos, u_neg, extra)
 
-        def matmul_road(slot):
-            x_sb = x_tiles[slot]
+        def matmul_road(i):
+            x_sb = x_tiles[i]
             u_pos = upool.tile([P, COLS], F32, name="u_pos")
             u_neg = upool.tile([P, COLS], F32, name="u_neg")
             up_v = u_pos[:].rearrange("p (s j c) -> p s j c", s=8, j=TILES)
@@ -178,14 +187,16 @@ def tile_hadlinear_t_kernel(tc, x, weight, out):
                     nc.scalar.copy(out=up_v[:, 4 * top : 4 * top + 4, j, :], in_=z_c)
                     if top == 1:
                         nc.scalar.mul(out=un_v[:, 4:8, j, :], in_=z_c, mul=-1.0)
-            u_tiles[slot] = (u_pos, u_neg, 2)
+            u_tiles[i] = (u_pos, u_neg, 2)
 
-        def adding_transposes(slot, follower):
-            u_pos, u_neg, extra = u_tiles[slot]
+        def adding_transposes(i, follower):
+            G, j0, n, unused = SLOTS[i]
+            u_pos, u_neg, extra = u_tiles[i]
+            width = n * P
             terms = 8 >> extra
             grp = gpool.tile([P, COLS], BF16, name="grp", align_bytes=64)
-            grp_v = grp[:].rearrange("p (j g m t) -> p j g m t", j=TILES, g=2, t=4)
-            for j in range(TILES):
+            grp_v = grp[:, : n * D].rearrange("p (j g m t) -> p j g m t", g=2, m=P, t=4)
+            for j in range(n):
                 banks = [psum_y.tile([P, 512], F32, tag="y", name="y_ps%d" % g) for g in range(2)]
                 for t in range(4):
                     for sg in range(terms):
@@ -195,7 +206,7 @@ def tile_hadlinear_t_kernel(tc, x, weight, out):
                             part = u_neg if minus(a8 >> extra, sg) else u_pos
                             nc.tensor.matmul(
                                 out=banks[g][:, P * t : P * t + P],
-                                lhsT=part[:, GROUP * s8 + P * j : GROUP * s8 + P * j + P],
+                                lhsT=part[:, width * s8 + P * j : width * s8 + P * j + P],
                                 rhs=ident[:],
                                 is_transpose=True,
                                 start=(sg == 0),
@@ -207,26 +218,31 @@ def tile_hadlinear_t_kernel(tc, x, weight, out):
                         in_=banks[g][:].rearrange("p (t m) -> p m t", t=4),
                         mul=0.0625,
                     )
-                if j == 1 and follower is not None:
+                if j == min(1, n - 1) and follower < n_slots:
                     negate(follower)
-            grp_tiles[slot] = grp
+            grp_tiles[i] = grp
 
-        def quantise(slot):
+        def quantise(i):
+            n = SLOTS[i][2]
             codes = work.tile([P, COLS // 4], U32, name="codes", align_bytes=64)
             scales = work.tile([P, COLS // 4], U8, name="scales", align_bytes=64)
             nc.vector.quantize_mx(
-                out=codes[:].bitcast(FP8X4), scales=scales[:], in_=grp_tiles[slot][:]
+                out=codes[:, : n * O].bitcast(FP8X4),
+                scales=scales[:, : n * O],
+                in_=grp_tiles[i][:, : n * D],
             )
-            code_tiles[slot] = (codes, scales)
+            code_tiles[i] = (codes, scales)
 
-        def linear(slot):
-            codes, scales = code_tiles[slot]
+        def linear(i):
+            G, j0, n, unused = SLOTS[i]
+            codes, scales = code_tiles[i]
             res = work.tile([P, TILES * O], F32, name="res")
-            for c in range(2):
+            for c in range(0, n, 2):
+                here = min(2, n - c)
                 o_ps = psum_o.tile([P, 512], F32, tag="o", name="o_ps")
-                for jj in range(2):
+                for jj in range(here):
                     for g in range(2):
-                        col = 256 * (2 * c + jj) + P * g
+                        col = 256 * (c + jj) + P * g
                         nc.tensor.matmul_mx(
                             out=o_ps[:, O * jj : O * jj + O],
                             lhsT=codes[:, col : col + P].bitcast(FP8X4),
@@ -236,11 +252,10 @@ def tile_hadlinear_t_kernel(tc, x, weight, out):
                             start=(g == 0),
                             stop=(g == 1),
                         )
-                nc.scalar.copy(out=res[:, 512 * c : 512 * c + 512], in_=o_ps[:])
-            nc.sync.dma_start(out=ov[slot], in_=res[:])
+                nc.scalar.copy(out=res[:, O * c : O * (c + here)], in_=o_ps[:, : O * here])
+            nc.sync.dma_start(out=ov[G][:, O * j0 : O * (j0 + n)], in_=res[:, : O * n])
 
-        first = N_MATMUL
-        vector_stages(first, 0, 4)
+        vector_stages(n_mm, 0, 4)
 
         w_r = const.tile([P, 2 * D], BF16)
         w_grp = const.tile([P, 2 * O * 4], BF16, align_bytes=64)
@@ -263,31 +278,26 @@ def tile_hadlinear_t_kernel(tc, x, weight, out):
         w_codes = const.tile([P, 2 * O], U32, align_bytes=64)
         w_scales = const.tile([P, 2 * O], U8, align_bytes=64)
 
-        for slot in range(N_MATMUL):
-            matmul_road(slot)
-            adding_transposes(slot, None)
-        load_x(first + 1)
-        vector_stages(first, 4, 5 + EXTRA[0])
+        for i in range(n_mm):
+            matmul_road(i)
+            adding_transposes(i, n_slots)
+        load_x(n_mm + 1)
+        vector_stages(n_mm, 4, 8)
         nc.vector.quantize_mx(out=w_codes[:].bitcast(FP8X4), scales=w_scales[:], in_=w_grp[:])
-        negate(first)
+        negate(n_mm)
 
-        for k in range(N_GROUPS - 1):
-            slot = first + k
-            nxt = slot + 1
-            if nxt + 1 < N_GROUPS:
-                load_x(nxt + 1)
-            if nxt < N_GROUPS:
-                vector_stages(nxt, 0, 1)
-            if k == 0:
+        for i in range(n_mm, n_slots + 2):
+            load_x(i + 2)
+            vector_stages(i + 1, 0, 1)
+            if i == n_mm:
                 ready = [0]
-            elif k == 1:
+            elif i == n_mm + 1:
                 ready = [1, 2]
             else:
-                ready = [k + 1]
+                ready = [i - 2]
             for done in ready:
                 quantise(done)
                 linear(done)
-            if nxt < N_GROUPS:
-                vector_stages(nxt, 1, 5 + EXTRA[nxt - N_MATMUL])
-            if slot < N_GROUPS:
-                adding_transposes(slot, nxt if nxt < N_GROUPS else None)
+            vector_stages(i + 1, 1, 8)
+            if i < n_slots:
+                adding_transposes(i, i + 1)

@@ -22,7 +22,7 @@ COLS = TILES * D
 FLOPS = 2 * TOKENS * D * O + TOKENS * D * 8
 
 MATMUL_SLOTS = [(0, 0, 4, None), (1, 0, 4, None), (2, 0, 4, None)]
-ADD_SLOTS = [(G, 0, 4, 0) for G in range(3, 15)] + [
+ADD_SLOTS = [(G, 0, 4, 1 if G == 8 else 0) for G in range(3, 15)] + [
     (15, 0, 1, 0),
     (15, 1, 1, 0),
     (15, 2, 1, 1),

from contextlib import ExitStack

import concourse.mybir as mybir
from concourse.masks import make_identity

F32 = mybir.dt.float32
BF16 = mybir.dt.bfloat16
U32 = mybir.dt.uint32
U8 = mybir.dt.uint8
FP8X4 = mybir.dt.float8_e4m3fn_x4
ALU = mybir.AluOpType

P = 128
TOKENS = 8192
D = 1024
O = 256
GROUP = 512
TILES = GROUP // P
N_GROUPS = TOKENS // GROUP
COLS = TILES * D

FLOPS = 2 * TOKENS * D * O + TOKENS * D * 8

MATMUL_SLOTS = [(0, 0, 4, None), (1, 0, 4, None), (2, 0, 4, None)]
ADD_SLOTS = [(G, 0, 4, 1 if G == 8 else 0) for G in range(3, 15)] + [
    (15, 0, 1, 0),
    (15, 1, 1, 0),
    (15, 2, 1, 1),
    (15, 3, 1, 2),
]
SLOTS = MATMUL_SLOTS + ADD_SLOTS


def minus(a, s):
    both = a & s
    return ((both >> 2) ^ (both >> 1) ^ both) & 1 == 1


def tile_hadlinear_t_kernel(tc, x, weight, out):
    nc = tc.nc
    xv = x.flatten_outer_dims().rearrange("(G p j) f -> G p (j f)", p=P, j=TILES)
    ov = out.flatten_outer_dims().rearrange("(G p j) o -> G p (j o)", p=P, j=TILES)
    n_mm = len(MATMUL_SLOTS)
    n_slots = len(SLOTS)

    with ExitStack() as ctx:
        const = ctx.enter_context(tc.tile_pool(name="const", bufs=1))
        xpool = ctx.enter_context(tc.tile_pool(name="xpool", bufs=4))
        stage = ctx.enter_context(tc.tile_pool(name="stage", bufs=1))
        upool = ctx.enter_context(tc.tile_pool(name="upool", bufs=3))
        gpool = ctx.enter_context(tc.tile_pool(name="gpool", bufs=3))
        work = ctx.enter_context(tc.tile_pool(name="work", bufs=2))
        psum_y = ctx.enter_context(tc.psum_pool(name="psum_y", bufs=6))
        psum_o = ctx.enter_context(tc.psum_pool(name="psum_o", bufs=2))
        ctx.enter_context(tc.manual_schedule())

        x_tiles = {}
        mid_tiles = {}
        u_tiles = {}
        grp_tiles = {}
        code_tiles = {}

        def load_x(i):
            if i >= n_slots:
                return
            G, j0, n, extra = SLOTS[i]
            x_sb = xpool.tile([P, COLS], BF16, name="x_sb")
            nc.sync.dma_start(out=x_sb[:, : n * D], in_=xv[G][:, j0 * D : (j0 + n) * D])
            x_tiles[i] = x_sb

        load_x(n_mm)
        load_x(0)
        w_sb = const.tile([P, 2 * D], BF16)
        nc.scalar.dma_start(
            out=w_sb[:].rearrange("p (a k) -> p a k", a=2),
            in_=weight.rearrange("(a p) k -> p a k", p=P),
        )
        load_x(1)
        load_x(2)

        ident = const.tile([P, P], F32)
        make_identity(nc, ident[:])
        ident_bf = const.tile([P, P], BF16)
        make_identity(nc, ident_bf[:])

        h_src = ident
        for st in range(7):
            h_dst = const.tile([P, P], F32, name="h_%d" % (st % 2))
            hp = h_src[:].rearrange("p (m two) -> p m two", two=2)
            nc.vector.tensor_tensor(out=h_dst[:, 0:64], in0=hp[:, :, 0], in1=hp[:, :, 1], op=ALU.add)
            nc.vector.tensor_tensor(
                out=h_dst[:, 64:128], in0=hp[:, :, 0], in1=hp[:, :, 1], op=ALU.subtract
            )
            h_src = h_dst
        h128 = const.tile([P, P], BF16)
        nc.vector.tensor_copy(out=h128[:], in_=h_src[:])

        def add_and_subtract(plus, less, in0, in1):
            nc.vector.tensor_tensor(out=plus, in0=in0, in1=in1, op=ALU.add)
            nc.vector.tensor_tensor(out=less, in0=in0, in1=in1, op=ALU.subtract)

        def vector_stages(i, first, last):
            if i >= n_slots:
                return
            G, j0, n, extra = SLOTS[i]
            cols = n * D
            for st in range(first, min(last, 5 + extra)):
                if st == 4 + extra:
                    dst = upool.tile([P, COLS], F32, name="u_pos")
                elif st % 2 == 0:
                    dst = stage.tile([P, COLS], F32, name="buf_a")
                else:
                    dst = stage.tile([P, COLS], F32, name="buf_b")
                if st < 5:
                    halves = dst[:, :cols].rearrange("p (r b m) -> p r b m", b=2, m=16)
                    if st == 0:
                        pairs = x_tiles[i][:, :cols].rearrange(
                            "p (q s m two) -> p s q m two", s=8, m=16, two=2
                        )
                        add_and_subtract(
                            halves[:, :, 0, :].rearrange("p (s q) m -> p s q m", s=8),
                            halves[:, :, 1, :].rearrange("p (s q) m -> p s q m", s=8),
                            pairs[:, :, :, :, 0],
                            pairs[:, :, :, :, 1],
                        )
                    else:
                        pairs = mid_tiles[i][:, :cols].rearrange(
                            "p (r m two) -> p r m two", m=16, two=2
                        )
                        add_and_subtract(
                            halves[:, :, 0, :], halves[:, :, 1, :], pairs[:, :, :, 0], pairs[:, :, :, 1]
                        )
                else:
                    run = (n * P) << (st - 5)
                    sv = mid_tiles[i][:, :cols].rearrange("p (h two c) -> p h two c", two=2, c=run)
                    dv = dst[:, :cols].rearrange("p (h two c) -> p h two c", two=2, c=run)
                    add_and_subtract(dv[:, :, 0, :], dv[:, :, 1, :], sv[:, :, 0, :], sv[:, :, 1, :])
                mid_tiles[i] = dst

        def negate(i):
            G, j0, n, extra = SLOTS[i]
            width = n * P
            u_pos = mid_tiles[i]
            u_neg = upool.tile([P, COLS], F32, name="u_neg")
            for lo in range(width << extra, 8 * width, 512):
                hi = min(lo + 512, 8 * width)
                nc.scalar.mul(out=u_neg[:, lo:hi], in_=u_pos[:, lo:hi], mul=-1.0)
            u_tiles[i] = (u_pos, u_neg, extra)

        def matmul_road(i):
            x_sb = x_tiles[i]
            u_pos = upool.tile([P, COLS], F32, name="u_pos")
            u_neg = upool.tile([P, COLS], F32, name="u_neg")
            up_v = u_pos[:].rearrange("p (s j c) -> p s j c", s=8, j=TILES)
            un_v = u_neg[:].rearrange("p (s j c) -> p s j c", s=8, j=TILES)
            xt_tiles = {}

            def transposes(j):
                xt_ps = psum_y.tile([P, D], BF16, tag="y", name="xt_ps")
                for c in range(8):
                    nc.tensor.transpose(
                        xt_ps[:, P * c : P * c + P],
                        x_sb[:, D * j + P * c : D * j + P * c + P],
                        ident_bf[:],
                    )
                xT_new = work.tile([P, D], BF16, name="xT")
                nc.scalar.copy(out=xT_new[:], in_=xt_ps[:])
                xt_tiles[j] = xT_new

            transposes(0)
            for j in range(TILES):
                if j + 1 < TILES:
                    transposes(j + 1)
                xT = xt_tiles[j]
                for top in range(2):
                    z_ps = psum_y.tile([P, 512], F32, tag="y", name="z_ps")
                    z_v = z_ps[:].rearrange("p (c b l) -> p c b l", c=4, b=4)
                    for b in range(4):
                        nc.tensor.matmul(
                            out=z_v[:, :, b, :],
                            lhsT=xT[:, P * (2 * b + top) : P * (2 * b + top) + P],
                            rhs=h128[:],
                            start=True,
                            stop=True,
                        )
                    z_c = z_ps[:].rearrange("p (c r) -> p c r", c=4)
                    nc.scalar.copy(out=up_v[:, 4 * top : 4 * top + 4, j, :], in_=z_c)
                    if top == 1:
                        nc.scalar.mul(out=un_v[:, 4:8, j, :], in_=z_c, mul=-1.0)
            u_tiles[i] = (u_pos, u_neg, 2)

        def adding_transposes(i, follower):
            G, j0, n, unused = SLOTS[i]
            u_pos, u_neg, extra = u_tiles[i]
            width = n * P
            terms = 8 >> extra
            grp = gpool.tile([P, COLS], BF16, name="grp", align_bytes=64)
            grp_v = grp[:, : n * D].rearrange("p (j g m t) -> p j g m t", g=2, m=P, t=4)
            for j in range(n):
                banks = [psum_y.tile([P, 512], F32, tag="y", name="y_ps%d" % g) for g in range(2)]
                for t in range(4):
                    for sg in range(terms):
                        for g in range(2):
                            a8 = 4 * g + t
                            s8 = (sg << extra) | (a8 & ((1 << extra) - 1))
                            part = u_neg if minus(a8 >> extra, sg) else u_pos
                            nc.tensor.matmul(
                                out=banks[g][:, P * t : P * t + P],
                                lhsT=part[:, width * s8 + P * j : width * s8 + P * j + P],
                                rhs=ident[:],
                                is_transpose=True,
                                start=(sg == 0),
                                stop=(sg == terms - 1),
                            )
                for g in range(2):
                    nc.scalar.mul(
                        out=grp_v[:, j, g, :, :],
                        in_=banks[g][:].rearrange("p (t m) -> p m t", t=4),
                        mul=0.0625,
                    )
                if j == min(1, n - 1) and follower < n_slots:
                    negate(follower)
            grp_tiles[i] = grp

        def quantise(i):
            n = SLOTS[i][2]
            codes = work.tile([P, COLS // 4], U32, name="codes", align_bytes=64)
            scales = work.tile([P, COLS // 4], U8, name="scales", align_bytes=64)
            nc.vector.quantize_mx(
                out=codes[:, : n * O].bitcast(FP8X4),
                scales=scales[:, : n * O],
                in_=grp_tiles[i][:, : n * D],
            )
            code_tiles[i] = (codes, scales)

        def linear(i):
            G, j0, n, unused = SLOTS[i]
            codes, scales = code_tiles[i]
            res = work.tile([P, TILES * O], F32, name="res")
            for c in range(0, n, 2):
                here = min(2, n - c)
                o_ps = psum_o.tile([P, 512], F32, tag="o", name="o_ps")
                for jj in range(here):
                    for g in range(2):
                        col = 256 * (c + jj) + P * g
                        nc.tensor.matmul_mx(
                            out=o_ps[:, O * jj : O * jj + O],
                            lhsT=codes[:, col : col + P].bitcast(FP8X4),
                            lhsT_scale=scales[:, col : col + P],
                            rhs=w_codes[:, O * g : O * g + O].bitcast(FP8X4),
                            rhs_scale=w_scales[:, O * g : O * g + O],
                            start=(g == 0),
                            stop=(g == 1),
                        )
                nc.scalar.copy(out=res[:, O * c : O * (c + here)], in_=o_ps[:, : O * here])
            nc.sync.dma_start(out=ov[G][:, O * j0 : O * (j0 + n)], in_=res[:, : O * n])

        vector_stages(n_mm, 0, 4)

        w_r = const.tile([P, 2 * D], BF16)
        w_grp = const.tile([P, 2 * O * 4], BF16, align_bytes=64)
        w_grp_v = w_grp[:].rearrange("p (g a o t) -> p g a o t", g=2, a=2, t=4)
        for a in range(2):
            nc.scalar.copy(
                out=w_r[:, D * a : D * a + D].rearrange("p (c b l) -> p c b l", c=8, b=4),
                in_=w_sb[:, D * a : D * a + D].rearrange("p (b c l) -> p c b l", c=8, b=4),
            )
            wt_ps = psum_o.tile([P, D], BF16, tag="o", name="wt_ps")
            for c in range(8):
                nc.tensor.transpose(
                    wt_ps[:, P * c : P * c + P],
                    w_r[:, D * a + P * c : D * a + P * c + P],
                    ident_bf[:],
                )
            wt_v = wt_ps[:].rearrange("p (g t o) -> p g o t", g=2, t=4)
            for g in range(2):
                nc.scalar.copy(out=w_grp_v[:, g, a, :, :], in_=wt_v[:, g, :, :])
        w_codes = const.tile([P, 2 * O], U32, align_bytes=64)
        w_scales = const.tile([P, 2 * O], U8, align_bytes=64)

        for i in range(n_mm):
            matmul_road(i)
            adding_transposes(i, n_slots)
        load_x(n_mm + 1)
        vector_stages(n_mm, 4, 8)
        nc.vector.quantize_mx(out=w_codes[:].bitcast(FP8X4), scales=w_scales[:], in_=w_grp[:])
        negate(n_mm)

        for i in range(n_mm, n_slots + 2):
            load_x(i + 2)
            vector_stages(i + 1, 0, 1)
            if i == n_mm:
                ready = [0]
            elif i == n_mm + 1:
                ready = [1, 2]
            else:
                ready = [i - 2]
            for done in ready:
                quantise(done)
                linear(done)
            vector_stages(i + 1, 1, 8)
            if i < n_slots:
                adding_transposes(i, i + 1)
